import numpy as np
import ml_dtypes


def mxq(x, axis, fmt="e4m3"):
    dtype, down = {"e4m3": (ml_dtypes.float8_e4m3fn, 7), "e5m2": (ml_dtypes.float8_e5m2, 14)}[fmt]
    v = np.moveaxis(np.asarray(x, np.float32).astype(ml_dtypes.bfloat16).astype(np.float64), axis, -1)
    blocks = v.reshape(v.shape[:-1] + (-1, 32))
    amax = np.abs(blocks).max(-1, keepdims=True)
    byte = np.maximum(np.where(amax > 0, np.frexp(amax)[1] - 1 + 127, 0) - down, 1)
    scale = np.exp2(byte - 127.0)
    codes = (blocks / scale).astype(np.float32).astype(dtype).astype(np.float64)
    return np.moveaxis((codes * scale).reshape(v.shape), -1, axis)


WIDE = False


def mx_kscale(k):
    if not WIDE:
        return np.ones(k)
    levels = np.array([10, -10, 5, -5, 0])
    a = np.random.permutation(np.resize(levels, k // 512 * 4)).reshape(k // 512, 4)
    idx = np.arange(k)
    return np.exp2(a[idx // 512, idx % 128 // 32])


BF16 = ml_dtypes.bfloat16


def bf(x):
    return np.asarray(x, np.float32).astype(BF16)


def f64(x):
    return np.asarray(x).astype(np.float64)


B, HW, C, HID, WS, SS, HEADS = 8, 32, 512, 2048, 8, 4, 16
L = HW * HW
NH = HW // WS
EPS = 1e-5


def adain(x, scale, shift):
    m = x.mean(2, keepdims=True)
    s = np.std(x, axis=2, keepdims=True, ddof=1) + EPS
    return (x - m) / s * scale + shift


def setup_inputs():
    s = mx_kscale(C)
    return {"o_attn": bf(0.4 * np.random.standard_normal((NH * NH * B, WS * WS, C)) * s),
            "out_w": bf(np.random.standard_normal((C, C)) / np.sqrt(C) / s[None, :]),
            "out_b": bf(0.1 * np.random.standard_normal(C)),
            "ada1_scale": bf(1.0 + 0.1 * np.random.standard_normal((1, L, 1))),
            "ada1_shift": bf(0.1 * np.random.standard_normal((1, L, 1))),
            "x": bf(np.random.standard_normal((B, L, C)))}


def reference(o_attn, out_w, out_b, ada1_scale, ada1_shift, x):
    a = (mxq(f64(o_attn), 2, "e4m3") @ mxq(f64(out_w), 1, "e4m3").T) + f64(out_b)
    a = np.swapaxes(a.reshape(B, NH, NH, WS, WS, C), 2, 3).reshape(B, HW, HW, C)
    a = np.roll(a, (SS, SS), axis=(1, 2)).reshape(B, L, C)
    return f64(x) + adain(a, f64(ada1_scale), f64(ada1_shift))

@@ -1,0 +1,187 @@
+from contextlib import ExitStack
+
+import concourse.mybir as mybir
+from concourse.masks import make_identity
+
+F32 = mybir.dt.float32
+BF16 = mybir.dt.bfloat16
+U32 = mybir.dt.uint32
+U8 = mybir.dt.uint8
+FP8X4 = mybir.dt.float8_e4m3fn_x4
+ALU = mybir.AluOpType
+ACT = mybir.ActivationFunctionType
+
+P = 128
+C = 512
+IMAGES = 8
+GRID = 32
+WS = 8
+NWIN = GRID // WS
+SHIFT = 4
+BLOCKS = 4
+EPS = 1e-5
+
+FLOPS = 2 * IMAGES * GRID * GRID * C * C
+
+
+def rolled(count, shift):
+    pieces = [(0, shift, count - shift)]
+    if shift:
+        pieces.append((count - shift, 0, shift))
+    return pieces
+
+
+def make_window_permutation(nc, perm, ident, carry):
+    dst = perm.rearrange("p (wi rh rl wj) -> p wi rh rl wj", wi=NWIN, rh=2, rl=SHIFT, wj=NWIN)
+    src = ident.rearrange("p (wi wj rh rl) -> p wi rh rl wj", wi=NWIN, wj=NWIN, rh=2, rl=SHIFT)
+    for rh in range(2):
+        for wi_src, wi_dst, wi_len in rolled(NWIN, rh):
+            for wj_src, wj_dst, wj_len in rolled(NWIN, carry):
+                nc.vector.tensor_copy(
+                    out=dst[:, wi_dst : wi_dst + wi_len, 1 - rh, :, wj_dst : wj_dst + wj_len],
+                    in_=src[:, wi_src : wi_src + wi_len, rh, :, wj_src : wj_src + wj_len],
+                )
+
+
+def transpose_and_quantise(nc, stage, turn, rows, perm, codes, scales):
+    grouped = stage.tile([P, BLOCKS * C], BF16, align_bytes=64)
+    grouped_words = grouped[:].bitcast(F32).rearrange("p (a j u) -> p a j u", a=BLOCKS, u=2)
+    for pair in range(BLOCKS // 2):
+        turned = turn.tile([P, 2, 2, P], F32)
+        for a in range(2):
+            words = rows[:, 2 * pair + a, :].bitcast(F32)
+            for u in range(2):
+                nc.tensor.transpose(turned[:, a, u, :], words[:, u * P : (u + 1) * P], perm)
+        nc.scalar.copy(
+            out=grouped_words[:, 2 * pair : 2 * pair + 2, :, :],
+            in_=turned[:].rearrange("p a u j -> p a j u"),
+        )
+    nc.vector.quantize_mx(out=codes.bitcast(FP8X4), scales=scales, in_=grouped[:])
+
+
+def tile_swintransformerblock_pb_t_kernel(
+    tc, o_attn, out_w, out_b, ada1_scale, ada1_shift, x, out
+):
+    nc = tc.nc
+    halves = 2 * IMAGES
+
+    o_rows = o_attn.flatten_outer_dims().rearrange("(b p c) k -> b p c k", p=P, c=WS)
+    x_rows = x.rearrange("b (p s) n -> b p s n", s=WS)
+    out_rows = out.rearrange("b (p s) n -> b p s n", s=WS)
+
+    with ExitStack() as stack:
+        consts = stack.enter_context(tc.tile_pool(name="consts", bufs=1))
+        resident = stack.enter_context(tc.tile_pool(name="resident", bufs=halves))
+        stage = stack.enter_context(tc.tile_pool(name="stage", bufs=2))
+        work = stack.enter_context(tc.tile_pool(name="work", bufs=3))
+        stats = stack.enter_context(tc.tile_pool(name="stats", bufs=4))
+        turn = stack.enter_context(tc.psum_pool(name="turn", bufs=4))
+        accs = stack.enter_context(tc.psum_pool(name="accs", bufs=4))
+
+        w_rows = consts.tile([P, BLOCKS, C], BF16)
+        nc.sync.dma_start(out=w_rows[:], in_=out_w.rearrange("(a p) k -> p a k", p=P))
+        o_tiles = []
+        x_tiles = []
+        for h in range(halves):
+            b, c_half = divmod(h, 2)
+            s_half = 1 - c_half
+            o_tile = resident.tile([P, BLOCKS, C], BF16)
+            nc.sync.dma_start(out=o_tile[:], in_=o_rows[b, :, BLOCKS * c_half : BLOCKS * (c_half + 1), :])
+            x_tile = resident.tile([P, BLOCKS, C], BF16)
+            nc.sync.dma_start(out=x_tile[:], in_=x_rows[b, :, BLOCKS * s_half : BLOCKS * (s_half + 1), :])
+            o_tiles.append(o_tile)
+            x_tiles.append(x_tile)
+
+        bias = consts.tile([P, C], BF16)
+        nc.scalar.dma_start(out=bias[:], in_=out_b.partition_broadcast(P))
+        gain_bf = consts.tile([P, WS], BF16)
+        nc.scalar.dma_start(out=gain_bf[:], in_=ada1_scale.flatten_outer_dims().rearrange("(p s) q -> p (s q)", p=P))
+        offset_bf = consts.tile([P, WS], BF16)
+        nc.scalar.dma_start(out=offset_bf[:], in_=ada1_shift.flatten_outer_dims().rearrange("(p s) q -> p (s q)", p=P))
+        gain = consts.tile([P, WS], F32)
+        nc.vector.tensor_copy(out=gain[:], in_=gain_bf[:])
+        offset = consts.tile([P, WS], F32)
+        nc.vector.tensor_copy(out=offset[:], in_=offset_bf[:])
+
+        ident = consts.tile([P, P], F32)
+        make_identity(nc, ident[:])
+        perms = []
+        for carry in range(2):
+            perm = consts.tile([P, P], F32, name="perm%d" % carry)
+            make_window_permutation(nc, perm[:], ident[:], carry)
+            perms.append(perm)
+
+        w_codes = consts.tile([P, C], U32, align_bytes=64)
+        w_scales = consts.tile([P, C], U8, align_bytes=64)
+        transpose_and_quantise(nc, stage, turn, w_rows, ident[:], w_codes[:], w_scales[:])
+
+        for h in range(halves):
+            b, c_half = divmod(h, 2)
+            s_half = 1 - c_half
+            slots = slice(BLOCKS * s_half, BLOCKS * (s_half + 1))
+
+            o_codes = stage.tile([P, BLOCKS * P], U32, align_bytes=64)
+            o_scales = stage.tile([P, BLOCKS * P], U8, align_bytes=64)
+            transpose_and_quantise(
+                nc, stage, turn, o_tiles[h], perms[c_half][:], o_codes[:], o_scales[:]
+            )
+
+            t_all = work.tile([P, BLOCKS, C], F32)
+            t_sum = stats.tile([P, BLOCKS], F32)
+            for a in range(BLOCKS):
+                cols = slice(a * P, (a + 1) * P)
+                acc = accs.tile([P, C], F32)
+                nc.tensor.matmul_mx(
+                    out=acc[:],
+                    lhsT=o_codes[:, cols].bitcast(FP8X4),
+                    lhsT_scale=o_scales[:, cols],
+                    rhs=w_codes[:].bitcast(FP8X4),
+                    rhs_scale=w_scales[:],
+                    start=True,
+                    stop=True,
+                )
+                nc.vector.scalar_tensor_tensor(
+                    out=t_all[:, a, :],
+                    in0=acc[:],
+                    scalar=1.0,
+                    in1=bias[:],
+                    op0=ALU.mult,
+                    op1=ALU.add,
+                    accum_out=t_sum[:, a : a + 1],
+                )
+
+            neg_mean = stats.tile([P, BLOCKS], F32)
+            nc.scalar.mul(out=neg_mean[:], in_=t_sum[:], mul=-1.0 / C)
+            squares = stage.tile([P, BLOCKS, C], BF16)
+            dev_sq = stats.tile([P, BLOCKS], F32)
+            for a in range(BLOCKS):
+                nc.scalar.activation(
+                    out=squares[:, a, :],
+                    in_=t_all[:, a, :],
+                    func=ACT.Square,
+                    bias=neg_mean[:, a : a + 1],
+                    scale=1.0,
+                    accum_out=dev_sq[:, a : a + 1],
+                )
+
+            std = stats.tile([P, BLOCKS], F32)
+            nc.scalar.activation(out=std[:], in_=dev_sq[:], func=ACT.Sqrt, scale=1.0 / (C - 1))
+            slope = stats.tile([P, BLOCKS], F32)
+            nc.vector.tensor_scalar_add(out=slope[:], in0=std[:], scalar1=EPS)
+            nc.vector.reciprocal(out=slope[:], in_=slope[:])
+            nc.vector.tensor_mul(out=slope[:], in0=slope[:], in1=gain[:, slots])
+            level = stats.tile([P, BLOCKS], F32)
+            nc.vector.tensor_mul(out=level[:], in0=neg_mean[:], in1=slope[:])
+            nc.vector.tensor_add(out=level[:], in0=level[:], in1=offset[:, slots])
+
+            result = work.tile([P, BLOCKS, C], F32)
+            for a in range(BLOCKS):
+                nc.scalar.activation(
+                    out=result[:, a, :],
+                    in_=t_all[:, a, :],
+                    func=ACT.Identity,
+                    bias=level[:, a : a + 1],
+                    scale=slope[:, a : a + 1],
+                )
+            nc.vector.tensor_add(out=result[:], in0=result[:], in1=x_tiles[h][:])
+            nc.gpsimd.dma_start(out=out_rows[b, :, slots, :], in_=result[:])

@@ -20,6 +20,7 @@ NWIN = GRID // WS
 SHIFT = 4
 BLOCKS = 4
 EPS = 1e-5
+VECTOR_SHARE = 1
 
 FLOPS = 2 * IMAGES * GRID * GRID * C * C
 
@@ -43,20 +44,29 @@ def make_window_permutation(nc, perm, ident, carry):
                 )
 
 
-def transpose_and_quantise(nc, stage, turn, rows, perm, codes, scales):
-    grouped = stage.tile([P, BLOCKS * C], BF16, align_bytes=64)
-    grouped_words = grouped[:].bitcast(F32).rearrange("p (a j u) -> p a j u", a=BLOCKS, u=2)
+def turn_rows(nc, turn, rows, perm):
+    banks = []
     for pair in range(BLOCKS // 2):
         turned = turn.tile([P, 2, 2, P], F32)
         for a in range(2):
             words = rows[:, 2 * pair + a, :].bitcast(F32)
             for u in range(2):
                 nc.tensor.transpose(turned[:, a, u, :], words[:, u * P : (u + 1) * P], perm)
-        nc.scalar.copy(
-            out=grouped_words[:, 2 * pair : 2 * pair + 2, :, :],
-            in_=turned[:].rearrange("p a u j -> p a j u"),
-        )
-    nc.vector.quantize_mx(out=codes.bitcast(FP8X4), scales=scales, in_=grouped[:])
+        banks.append(turned)
+    return banks
+
+
+def new_grouped(stage):
+    grouped = stage.tile([P, BLOCKS * C], BF16, align_bytes=64)
+    return grouped
+
+
+def group_words(copy_out, grouped, banks, pair):
+    grouped_words = grouped[:].bitcast(F32).rearrange("p (a j u) -> p a j u", a=BLOCKS, u=2)
+    copy_out(
+        out=grouped_words[:, 2 * pair : 2 * pair + 2, :, :],
+        in_=banks[pair][:].rearrange("p a u j -> p a j u"),
+    )
 
 
 def tile_swintransformerblock_pb_t_kernel(
@@ -69,6 +79,10 @@ def tile_swintransformerblock_pb_t_kernel(
     x_rows = x.rearrange("b (p s) n -> b p s n", s=WS)
     out_rows = out.rearrange("b (p s) n -> b p s n", s=WS)
 
+    def out_slots(h):
+        s_half = 1 - h % 2
+        return slice(BLOCKS * s_half, BLOCKS * (s_half + 1))
+
     with ExitStack() as stack:
         consts = stack.enter_context(tc.tile_pool(name="consts", bufs=1))
         resident = stack.enter_context(tc.tile_pool(name="resident", bufs=halves))
@@ -77,31 +91,33 @@ def tile_swintransformerblock_pb_t_kernel(
         stats = stack.enter_context(tc.tile_pool(name="stats", bufs=4))
         turn = stack.enter_context(tc.psum_pool(name="turn", bufs=4))
         accs = stack.enter_context(tc.psum_pool(name="accs", bufs=4))
+        stack.enter_context(tc.manual_schedule())
 
         w_rows = consts.tile([P, BLOCKS, C], BF16)
         nc.sync.dma_start(out=w_rows[:], in_=out_w.rearrange("(a p) k -> p a k", p=P))
         o_tiles = []
         x_tiles = []
         for h in range(halves):
-            b, c_half = divmod(h, 2)
-            s_half = 1 - c_half
+            c_half = h % 2
             o_tile = resident.tile([P, BLOCKS, C], BF16)
-            nc.sync.dma_start(out=o_tile[:], in_=o_rows[b, :, BLOCKS * c_half : BLOCKS * (c_half + 1), :])
+            nc.sync.dma_start(
+                out=o_tile[:], in_=o_rows[h // 2, :, BLOCKS * c_half : BLOCKS * (c_half + 1), :]
+            )
             x_tile = resident.tile([P, BLOCKS, C], BF16)
-            nc.sync.dma_start(out=x_tile[:], in_=x_rows[b, :, BLOCKS * s_half : BLOCKS * (s_half + 1), :])
+            nc.sync.dma_start(out=x_tile[:], in_=x_rows[h // 2, :, out_slots(h), :])
             o_tiles.append(o_tile)
             x_tiles.append(x_tile)
 
         bias = consts.tile([P, C], BF16)
         nc.scalar.dma_start(out=bias[:], in_=out_b.partition_broadcast(P))
         gain_bf = consts.tile([P, WS], BF16)
-        nc.scalar.dma_start(out=gain_bf[:], in_=ada1_scale.flatten_outer_dims().rearrange("(p s) q -> p (s q)", p=P))
+        nc.scalar.dma_start(
+            out=gain_bf[:], in_=ada1_scale.flatten_outer_dims().rearrange("(p s) q -> p (s q)", p=P)
+        )
         offset_bf = consts.tile([P, WS], BF16)
-        nc.scalar.dma_start(out=offset_bf[:], in_=ada1_shift.flatten_outer_dims().rearrange("(p s) q -> p (s q)", p=P))
-        gain = consts.tile([P, WS], F32)
-        nc.vector.tensor_copy(out=gain[:], in_=gain_bf[:])
-        offset = consts.tile([P, WS], F32)
-        nc.vector.tensor_copy(out=offset[:], in_=offset_bf[:])
+        nc.scalar.dma_start(
+            out=offset_bf[:], in_=ada1_shift.flatten_outer_dims().rearrange("(p s) q -> p (s q)", p=P)
+        )
 
         ident = consts.tile([P, P], F32)
         make_identity(nc, ident[:])
@@ -113,75 +129,171 @@ def tile_swintransformerblock_pb_t_kernel(
 
         w_codes = consts.tile([P, C], U32, align_bytes=64)
         w_scales = consts.tile([P, C], U8, align_bytes=64)
-        transpose_and_quantise(nc, stage, turn, w_rows, ident[:], w_codes[:], w_scales[:])
+        w_banks = turn_rows(nc, turn, w_rows, ident[:])
+        w_grouped = new_grouped(stage)
+        for pair in range(BLOCKS // 2):
+            group_words(nc.vector.tensor_copy, w_grouped, w_banks, pair)
+        nc.vector.quantize_mx(out=w_codes[:].bitcast(FP8X4), scales=w_scales[:], in_=w_grouped[:])
 
-        for h in range(halves):
-            b, c_half = divmod(h, 2)
-            s_half = 1 - c_half
-            slots = slice(BLOCKS * s_half, BLOCKS * (s_half + 1))
+        gain = consts.tile([P, WS], F32)
+        nc.vector.tensor_copy(out=gain[:], in_=gain_bf[:])
+        offset = consts.tile([P, WS], F32)
+        nc.vector.tensor_copy(out=offset[:], in_=offset_bf[:])
 
+        kept = {}
+
+        def turn_half(h):
+            kept["banks", h] = turn_rows(nc, turn, o_tiles[h], perms[h % 2][:])
+
+        def group_bank(h, pair):
+            if pair == 0:
+                kept["grouped", h] = new_grouped(stage)
+            group_words(nc.scalar.copy, kept["grouped", h], kept["banks", h], pair)
+
+        def quantise_half(h):
             o_codes = stage.tile([P, BLOCKS * P], U32, align_bytes=64)
             o_scales = stage.tile([P, BLOCKS * P], U8, align_bytes=64)
-            transpose_and_quantise(
-                nc, stage, turn, o_tiles[h], perms[c_half][:], o_codes[:], o_scales[:]
+            nc.vector.quantize_mx(
+                out=o_codes[:].bitcast(FP8X4), scales=o_scales[:], in_=kept["grouped", h][:]
             )
+            kept["codes", h] = o_codes
+            kept["scales", h] = o_scales
 
+        def project_block(h, a):
+            cols = slice(a * P, (a + 1) * P)
+            acc = accs.tile([P, C], F32)
+            nc.tensor.matmul_mx(
+                out=acc[:],
+                lhsT=kept["codes", h][:, cols].bitcast(FP8X4),
+                lhsT_scale=kept["scales", h][:, cols],
+                rhs=w_codes[:].bitcast(FP8X4),
+                rhs_scale=w_scales[:],
+                start=True,
+                stop=True,
+            )
+            kept["acc", h, a] = acc
+
+        def new_projection(h):
             t_all = work.tile([P, BLOCKS, C], F32)
             t_sum = stats.tile([P, BLOCKS], F32)
-            for a in range(BLOCKS):
-                cols = slice(a * P, (a + 1) * P)
-                acc = accs.tile([P, C], F32)
-                nc.tensor.matmul_mx(
-                    out=acc[:],
-                    lhsT=o_codes[:, cols].bitcast(FP8X4),
-                    lhsT_scale=o_scales[:, cols],
-                    rhs=w_codes[:].bitcast(FP8X4),
-                    rhs_scale=w_scales[:],
-                    start=True,
-                    stop=True,
-                )
-                nc.vector.scalar_tensor_tensor(
-                    out=t_all[:, a, :],
-                    in0=acc[:],
-                    scalar=1.0,
-                    in1=bias[:],
-                    op0=ALU.mult,
-                    op1=ALU.add,
-                    accum_out=t_sum[:, a : a + 1],
-                )
+            kept["t", h] = t_all
+            kept["t_sum", h] = t_sum
 
-            neg_mean = stats.tile([P, BLOCKS], F32)
-            nc.scalar.mul(out=neg_mean[:], in_=t_sum[:], mul=-1.0 / C)
+        def add_bias_block(h, a):
+            nc.vector.scalar_tensor_tensor(
+                out=kept["t", h][:, a, :],
+                in0=kept["acc", h, a][:],
+                scalar=1.0,
+                in1=bias[:],
+                op0=ALU.mult,
+                op1=ALU.add,
+                accum_out=kept["t_sum", h][:, a : a + 1],
+            )
+
+        def squared_deviations(h):
             squares = stage.tile([P, BLOCKS, C], BF16)
             dev_sq = stats.tile([P, BLOCKS], F32)
             for a in range(BLOCKS):
                 nc.scalar.activation(
                     out=squares[:, a, :],
-                    in_=t_all[:, a, :],
+                    in_=kept["t", h][:, a, :],
                     func=ACT.Square,
-                    bias=neg_mean[:, a : a + 1],
-                    scale=1.0,
+                    bias=kept["t_sum", h][:, a : a + 1],
+                    scale=-1.0 * C,
                     accum_out=dev_sq[:, a : a + 1],
                 )
+            kept["dev_sq", h] = dev_sq
 
+        def standard_deviation(h):
             std = stats.tile([P, BLOCKS], F32)
-            nc.scalar.activation(out=std[:], in_=dev_sq[:], func=ACT.Sqrt, scale=1.0 / (C - 1))
-            slope = stats.tile([P, BLOCKS], F32)
-            nc.vector.tensor_scalar_add(out=slope[:], in0=std[:], scalar1=EPS)
-            nc.vector.reciprocal(out=slope[:], in_=slope[:])
-            nc.vector.tensor_mul(out=slope[:], in0=slope[:], in1=gain[:, slots])
-            level = stats.tile([P, BLOCKS], F32)
-            nc.vector.tensor_mul(out=level[:], in0=neg_mean[:], in1=slope[:])
-            nc.vector.tensor_add(out=level[:], in0=level[:], in1=offset[:, slots])
+            nc.scalar.activation(
+                out=std[:], in_=kept["dev_sq", h][:], func=ACT.Sqrt, scale=1.0 / ((C - 1) * C * C)
+            )
+            kept["std", h] = std
 
+        def slope_step(h, step):
+            if step == 0:
+                slope = stats.tile([P, BLOCKS], F32)
+                level = stats.tile([P, BLOCKS], F32)
+                kept["slope", h] = slope
+                kept["level", h] = level
+                nc.vector.tensor_scalar_add(out=slope[:], in0=kept["std", h][:], scalar1=EPS)
+            slope = kept["slope", h]
+            level = kept["level", h]
+            if step == 1:
+                nc.vector.reciprocal(out=slope[:], in_=slope[:])
+            if step == 2:
+                nc.vector.tensor_mul(out=slope[:], in0=slope[:], in1=gain[:, out_slots(h)])
+            if step == 3:
+                nc.vector.tensor_mul(out=level[:], in0=kept["t_sum", h][:], in1=slope[:])
+            if step == 4:
+                nc.vector.scalar_tensor_tensor(
+                    out=level[:],
+                    in0=level[:],
+                    scalar=-1.0 / C,
+                    in1=offset[:, out_slots(h)],
+                    op0=ALU.mult,
+                    op1=ALU.add,
+                )
+
+        def normalise(h):
             result = work.tile([P, BLOCKS, C], F32)
-            for a in range(BLOCKS):
+            for a in range(BLOCKS - VECTOR_SHARE):
                 nc.scalar.activation(
                     out=result[:, a, :],
-                    in_=t_all[:, a, :],
+                    in_=kept["t", h][:, a, :],
                     func=ACT.Identity,
-                    bias=level[:, a : a + 1],
-                    scale=slope[:, a : a + 1],
+                    bias=kept["level", h][:, a : a + 1],
+                    scale=kept["slope", h][:, a : a + 1],
                 )
+            kept["result", h] = result
+
+        def normalise_on_vector(h):
+            for a in range(BLOCKS - VECTOR_SHARE, BLOCKS):
+                nc.vector.tensor_scalar(
+                    out=kept["result", h][:, a, :],
+                    in0=kept["t", h][:, a, :],
+                    scalar1=kept["slope", h][:, a : a + 1],
+                    scalar2=kept["level", h][:, a : a + 1],
+                    op0=ALU.mult,
+                    op1=ALU.add,
+                )
+
+        def add_residual_and_store(h):
+            result = kept["result", h]
             nc.vector.tensor_add(out=result[:], in0=result[:], in1=x_tiles[h][:])
-            nc.gpsimd.dma_start(out=out_rows[b, :, slots, :], in_=result[:])
+            nc.gpsimd.dma_start(out=out_rows[h // 2, :, out_slots(h), :], in_=result[:])
+
+        def valid(h):
+            return 0 <= h < halves
+
+        for i in range(-3, halves + 2):
+            if valid(i + 3):
+                turn_half(i + 3)
+            if valid(i - 1):
+                squared_deviations(i - 1)
+            if valid(i + 2):
+                group_bank(i + 2, 0)
+            if valid(i - 1):
+                standard_deviation(i - 1)
+            if valid(i + 2):
+                group_bank(i + 2, 1)
+            if valid(i - 2):
+                normalise(i - 2)
+            if valid(i):
+                new_projection(i)
+            for a in range(BLOCKS):
+                if valid(i):
+                    add_bias_block(i, a)
+                if valid(i + 1):
+                    project_block(i + 1, a)
+                if valid(i - 1):
+                    slope_step(i - 1, a)
+            if valid(i - 2):
+                normalise_on_vector(i - 2)
+            if valid(i - 1):
+                slope_step(i - 1, BLOCKS)
+            if valid(i + 2):
+                quantise_half(i + 2)
+            if valid(i - 2):
+                add_residual_and_store(i - 2)

@@ -262,7 +262,7 @@ def tile_swintransformerblock_pb_t_kernel(
         def add_residual_and_store(h):
             result = kept["result", h]
             nc.vector.tensor_add(out=result[:], in0=result[:], in1=x_tiles[h][:])
-            nc.gpsimd.dma_start(out=out_rows[h // 2, :, out_slots(h), :], in_=result[:])
+            nc.sync.dma_start(out=out_rows[h // 2, :, out_slots(h), :], in_=result[:])
 
         def valid(h):
             return 0 <= h < halves

@@ -20,7 +20,11 @@ NWIN = GRID // WS
 SHIFT = 4
 BLOCKS = 4
 EPS = 1e-5
-VECTOR_SHARE = 1
+FIRST_ROUND = -3
+O_AHEAD = 6
+X_AHEAD = 2
+SHARED_BLOCKS = BLOCKS - 1
+SLOPE_STEPS = 5
 
 FLOPS = 2 * IMAGES * GRID * GRID * C * C
 
@@ -95,18 +99,24 @@ def tile_swintransformerblock_pb_t_kernel(
 
         w_rows = consts.tile([P, BLOCKS, C], BF16)
         nc.sync.dma_start(out=w_rows[:], in_=out_w.rearrange("(a p) k -> p a k", p=P))
-        o_tiles = []
-        x_tiles = []
-        for h in range(halves):
+        o_tiles = {}
+        x_tiles = {}
+
+        def load_o(h):
             c_half = h % 2
             o_tile = resident.tile([P, BLOCKS, C], BF16)
             nc.sync.dma_start(
                 out=o_tile[:], in_=o_rows[h // 2, :, BLOCKS * c_half : BLOCKS * (c_half + 1), :]
             )
+            o_tiles[h] = o_tile
+
+        def load_x(h):
             x_tile = resident.tile([P, BLOCKS, C], BF16)
             nc.sync.dma_start(out=x_tile[:], in_=x_rows[h // 2, :, out_slots(h), :])
-            o_tiles.append(o_tile)
-            x_tiles.append(x_tile)
+            x_tiles[h] = x_tile
+
+        for h in range(O_AHEAD + FIRST_ROUND):
+            load_o(h)
 
         bias = consts.tile([P, C], BF16)
         nc.scalar.dma_start(out=bias[:], in_=out_b.partition_broadcast(P))
@@ -238,7 +248,7 @@ def tile_swintransformerblock_pb_t_kernel(
 
         def normalise(h):
             result = work.tile([P, BLOCKS, C], F32)
-            for a in range(BLOCKS - VECTOR_SHARE):
+            for a in range(SHARED_BLOCKS):
                 nc.scalar.activation(
                     out=result[:, a, :],
                     in_=kept["t", h][:, a, :],
@@ -248,26 +258,34 @@ def tile_swintransformerblock_pb_t_kernel(
                 )
             kept["result", h] = result
 
-        def normalise_on_vector(h):
-            for a in range(BLOCKS - VECTOR_SHARE, BLOCKS):
-                nc.vector.tensor_scalar(
-                    out=kept["result", h][:, a, :],
-                    in0=kept["t", h][:, a, :],
-                    scalar1=kept["slope", h][:, a : a + 1],
-                    scalar2=kept["level", h][:, a : a + 1],
-                    op0=ALU.mult,
-                    op1=ALU.add,
-                )
-
-        def add_residual_and_store(h):
+        def finish_last_block(h):
+            last = BLOCKS - 1
             result = kept["result", h]
-            nc.vector.tensor_add(out=result[:], in0=result[:], in1=x_tiles[h][:])
-            nc.sync.dma_start(out=out_rows[h // 2, :, out_slots(h), :], in_=result[:])
+            nc.gpsimd.tensor_scalar(
+                out=result[:, last, :],
+                in0=kept["t", h][:, last, :],
+                scalar1=kept["slope", h][:, last : last + 1],
+                scalar2=kept["level", h][:, last : last + 1],
+                op0=ALU.mult,
+                op1=ALU.add,
+            )
+            nc.gpsimd.tensor_add(out=result[:, last, :], in0=result[:, last, :], in1=x_tiles[h][:, last, :])
+
+        def add_residual_block(h, a):
+            result = kept["result", h]
+            nc.vector.tensor_add(out=result[:, a, :], in0=result[:, a, :], in1=x_tiles[h][:, a, :])
+
+        def store(h):
+            nc.sync.dma_start(out=out_rows[h // 2, :, out_slots(h), :], in_=kept["result", h][:])
 
         def valid(h):
             return 0 <= h < halves
 
-        for i in range(-3, halves + 2):
+        for i in range(FIRST_ROUND, halves + 2):
+            if valid(i + O_AHEAD):
+                load_o(i + O_AHEAD)
+            if valid(i + X_AHEAD):
+                load_x(i + X_AHEAD)
             if valid(i + 3):
                 turn_half(i + 3)
             if valid(i - 1):
@@ -280,6 +298,7 @@ def tile_swintransformerblock_pb_t_kernel(
                 group_bank(i + 2, 1)
             if valid(i - 2):
                 normalise(i - 2)
+                finish_last_block(i - 2)
             if valid(i):
                 new_projection(i)
             for a in range(BLOCKS):
@@ -287,13 +306,12 @@ def tile_swintransformerblock_pb_t_kernel(
                     add_bias_block(i, a)
                 if valid(i + 1):
                     project_block(i + 1, a)
+            for step in range(SLOPE_STEPS):
                 if valid(i - 1):
-                    slope_step(i - 1, a)
+                    slope_step(i - 1, step)
+                if step == 0 and valid(i + 2):
+                    quantise_half(i + 2)
+                if 1 <= step <= SHARED_BLOCKS and valid(i - 2):
+                    add_residual_block(i - 2, step - 1)
             if valid(i - 2):
-                normalise_on_vector(i - 2)
-            if valid(i - 1):
-                slope_step(i - 1, BLOCKS)
-            if valid(i + 2):
-                quantise_half(i + 2)
-            if valid(i - 2):
-                add_residual_and_store(i - 2)
+                store(i - 2)

@@ -19,12 +19,14 @@ WS = 8
 NWIN = GRID // WS
 SHIFT = 4
 BLOCKS = 4
+PAIRS = BLOCKS // 2
 EPS = 1e-5
-FIRST_ROUND = -3
-O_AHEAD = 6
-X_AHEAD = 2
 SHARED_BLOCKS = BLOCKS - 1
-SLOPE_STEPS = 5
+FIRST_ROUND = -2
+LAST_LAG = 2
+O_AHEAD = 5
+X_AHEAD = 2
+LOAD_BUFS = 6
 
 FLOPS = 2 * IMAGES * GRID * GRID * C * C
 
@@ -60,16 +62,20 @@ def turn_rows(nc, turn, rows, perm):
     return banks
 
 
-def new_grouped(stage):
-    grouped = stage.tile([P, BLOCKS * C], BF16, align_bytes=64)
-    return grouped
-
-
 def group_words(copy_out, grouped, banks, pair):
     grouped_words = grouped[:].bitcast(F32).rearrange("p (a j u) -> p a j u", a=BLOCKS, u=2)
     copy_out(
         out=grouped_words[:, 2 * pair : 2 * pair + 2, :, :],
         in_=banks[pair][:].rearrange("p a u j -> p a j u"),
+    )
+
+
+def quantise_pair(nc, grouped, codes, scales, pair):
+    cols = slice(2 * P * pair, 2 * P * (pair + 1))
+    nc.vector.quantize_mx(
+        out=codes[:, cols].bitcast(FP8X4),
+        scales=scales[:, cols],
+        in_=grouped[:, 2 * C * pair : 2 * C * (pair + 1)],
     )
 
 
@@ -83,13 +89,15 @@ def tile_swintransformerblock_pb_t_kernel(
     x_rows = x.rearrange("b (p s) n -> b p s n", s=WS)
     out_rows = out.rearrange("b (p s) n -> b p s n", s=WS)
 
+    def first_out_slot(h):
+        return BLOCKS * (1 - h % 2)
+
     def out_slots(h):
-        s_half = 1 - h % 2
-        return slice(BLOCKS * s_half, BLOCKS * (s_half + 1))
+        return slice(first_out_slot(h), first_out_slot(h) + BLOCKS)
 
     with ExitStack() as stack:
         consts = stack.enter_context(tc.tile_pool(name="consts", bufs=1))
-        resident = stack.enter_context(tc.tile_pool(name="resident", bufs=halves))
+        loads = stack.enter_context(tc.tile_pool(name="loads", bufs=LOAD_BUFS))
         stage = stack.enter_context(tc.tile_pool(name="stage", bufs=2))
         work = stack.enter_context(tc.tile_pool(name="work", bufs=3))
         stats = stack.enter_context(tc.tile_pool(name="stats", bufs=4))
@@ -97,37 +105,39 @@ def tile_swintransformerblock_pb_t_kernel(
         accs = stack.enter_context(tc.psum_pool(name="accs", bufs=4))
         stack.enter_context(tc.manual_schedule())
 
-        w_rows = consts.tile([P, BLOCKS, C], BF16)
-        nc.sync.dma_start(out=w_rows[:], in_=out_w.rearrange("(a p) k -> p a k", p=P))
-        o_tiles = {}
-        x_tiles = {}
+        kept = {}
 
         def load_o(h):
-            c_half = h % 2
-            o_tile = resident.tile([P, BLOCKS, C], BF16)
-            nc.sync.dma_start(
-                out=o_tile[:], in_=o_rows[h // 2, :, BLOCKS * c_half : BLOCKS * (c_half + 1), :]
-            )
-            o_tiles[h] = o_tile
+            o_tile = loads.tile([P, BLOCKS, C], BF16)
+            first = BLOCKS * (h % 2)
+            nc.sync.dma_start(out=o_tile[:], in_=o_rows[h // 2, :, first : first + BLOCKS, :])
+            kept["o", h] = o_tile
 
         def load_x(h):
-            x_tile = resident.tile([P, BLOCKS, C], BF16)
+            x_tile = loads.tile([P, BLOCKS, C], BF16)
             nc.sync.dma_start(out=x_tile[:], in_=x_rows[h // 2, :, out_slots(h), :])
-            x_tiles[h] = x_tile
+            kept["x", h] = x_tile
 
+        w_rows = consts.tile([P, BLOCKS, C], BF16)
+        nc.sync.dma_start(out=w_rows[:], in_=out_w.rearrange("(a p) k -> p a k", p=P))
+        bias_row = consts.tile([P, C], BF16)
+        nc.vector.memset(bias_row[:], 0.0)
+        nc.sync.dma_start(out=bias_row[0:1, :], in_=out_b.rearrange("(o n) -> o n", o=1))
         for h in range(O_AHEAD + FIRST_ROUND):
             load_o(h)
+        gain = consts.tile([P, WS], BF16)
+        nc.sync.dma_start(
+            out=gain[:], in_=ada1_scale.flatten_outer_dims().rearrange("(p s) q -> p (s q)", p=P)
+        )
+        offset = consts.tile([P, WS], BF16)
+        nc.sync.dma_start(
+            out=offset[:], in_=ada1_shift.flatten_outer_dims().rearrange("(p s) q -> p (s q)", p=P)
+        )
 
-        bias = consts.tile([P, C], BF16)
-        nc.scalar.dma_start(out=bias[:], in_=out_b.partition_broadcast(P))
-        gain_bf = consts.tile([P, WS], BF16)
-        nc.scalar.dma_start(
-            out=gain_bf[:], in_=ada1_scale.flatten_outer_dims().rearrange("(p s) q -> p (s q)", p=P)
-        )
-        offset_bf = consts.tile([P, WS], BF16)
-        nc.scalar.dma_start(
-            out=offset_bf[:], in_=ada1_shift.flatten_outer_dims().rearrange("(p s) q -> p (s q)", p=P)
-        )
+        ones = consts.tile([P, P], BF16)
+        nc.vector.memset(ones[:], 1.0)
+        table_warmer = consts.tile([P, 1], F32)
+        nc.scalar.activation(out=table_warmer[:], in_=ones[:, 0:1], func=ACT.Sqrt)
 
         ident = consts.tile([P, P], F32)
         make_identity(nc, ident[:])
@@ -140,65 +150,64 @@ def tile_swintransformerblock_pb_t_kernel(
         w_codes = consts.tile([P, C], U32, align_bytes=64)
         w_scales = consts.tile([P, C], U8, align_bytes=64)
         w_banks = turn_rows(nc, turn, w_rows, ident[:])
-        w_grouped = new_grouped(stage)
-        for pair in range(BLOCKS // 2):
+        w_grouped = stage.tile([P, BLOCKS * C], BF16, align_bytes=64, tag="grouped")
+        for pair in range(PAIRS):
             group_words(nc.vector.tensor_copy, w_grouped, w_banks, pair)
-        nc.vector.quantize_mx(out=w_codes[:].bitcast(FP8X4), scales=w_scales[:], in_=w_grouped[:])
+        for pair in range(PAIRS):
+            quantise_pair(nc, w_grouped, w_codes, w_scales, pair)
 
-        gain = consts.tile([P, WS], F32)
-        nc.vector.tensor_copy(out=gain[:], in_=gain_bf[:])
-        offset = consts.tile([P, WS], F32)
-        nc.vector.tensor_copy(out=offset[:], in_=offset_bf[:])
-
-        kept = {}
+        bias_bank = accs.tile([P, C], F32, tag="acc")
+        nc.tensor.matmul(bias_bank[:], lhsT=ones[:], rhs=bias_row[:], start=True, stop=True)
+        bias = consts.tile([P, C], F32)
+        nc.vector.tensor_copy(out=bias[:], in_=bias_bank[:])
 
         def turn_half(h):
-            kept["banks", h] = turn_rows(nc, turn, o_tiles[h], perms[h % 2][:])
+            kept["banks", h] = turn_rows(nc, turn, kept["o", h], perms[h % 2][:])
 
         def group_bank(h, pair):
             if pair == 0:
-                kept["grouped", h] = new_grouped(stage)
+                grouped = stage.tile([P, BLOCKS * C], BF16, align_bytes=64, tag="grouped")
+                kept["grouped", h] = grouped
             group_words(nc.scalar.copy, kept["grouped", h], kept["banks", h], pair)
 
-        def quantise_half(h):
-            o_codes = stage.tile([P, BLOCKS * P], U32, align_bytes=64)
-            o_scales = stage.tile([P, BLOCKS * P], U8, align_bytes=64)
-            nc.vector.quantize_mx(
-                out=o_codes[:].bitcast(FP8X4), scales=o_scales[:], in_=kept["grouped", h][:]
-            )
-            kept["codes", h] = o_codes
-            kept["scales", h] = o_scales
+        def quantise(h, pair):
+            if pair == 0:
+                o_codes = stage.tile([P, BLOCKS * P], U32, align_bytes=64)
+                o_scales = stage.tile([P, BLOCKS * P], U8, align_bytes=64)
+                kept["codes", h] = o_codes
+                kept["scales", h] = o_scales
+            quantise_pair(nc, kept["grouped", h], kept["codes", h], kept["scales", h], pair)
 
-        def project_block(h, a):
-            cols = slice(a * P, (a + 1) * P)
-            acc = accs.tile([P, C], F32)
-            nc.tensor.matmul_mx(
-                out=acc[:],
-                lhsT=kept["codes", h][:, cols].bitcast(FP8X4),
-                lhsT_scale=kept["scales", h][:, cols],
-                rhs=w_codes[:].bitcast(FP8X4),
-                rhs_scale=w_scales[:],
-                start=True,
-                stop=True,
-            )
-            kept["acc", h, a] = acc
+        def project(h):
+            for a in range(BLOCKS):
+                cols = slice(a * P, (a + 1) * P)
+                acc = accs.tile([P, C], F32, tag="acc")
+                nc.tensor.matmul_mx(
+                    out=acc[:],
+                    lhsT=kept["codes", h][:, cols].bitcast(FP8X4),
+                    lhsT_scale=kept["scales", h][:, cols],
+                    rhs=w_codes[:].bitcast(FP8X4),
+                    rhs_scale=w_scales[:],
+                    start=True,
+                    stop=True,
+                )
+                kept["acc", h, a] = acc
 
-        def new_projection(h):
+        def add_bias(h):
             t_all = work.tile([P, BLOCKS, C], F32)
             t_sum = stats.tile([P, BLOCKS], F32)
+            for a in range(BLOCKS):
+                nc.vector.scalar_tensor_tensor(
+                    out=t_all[:, a, :],
+                    in0=kept["acc", h, a][:],
+                    scalar=1.0,
+                    in1=bias[:],
+                    op0=ALU.mult,
+                    op1=ALU.add,
+                    accum_out=t_sum[:, a : a + 1],
+                )
             kept["t", h] = t_all
             kept["t_sum", h] = t_sum
-
-        def add_bias_block(h, a):
-            nc.vector.scalar_tensor_tensor(
-                out=kept["t", h][:, a, :],
-                in0=kept["acc", h, a][:],
-                scalar=1.0,
-                in1=bias[:],
-                op0=ALU.mult,
-                op1=ALU.add,
-                accum_out=kept["t_sum", h][:, a : a + 1],
-            )
 
         def squared_deviations(h):
             squares = stage.tile([P, BLOCKS, C], BF16)
@@ -269,49 +278,46 @@ def tile_swintransformerblock_pb_t_kernel(
                 op0=ALU.mult,
                 op1=ALU.add,
             )
-            nc.gpsimd.tensor_add(out=result[:, last, :], in0=result[:, last, :], in1=x_tiles[h][:, last, :])
+            nc.gpsimd.tensor_add(
+                out=result[:, last, :], in0=result[:, last, :], in1=kept["x", h][:, last, :]
+            )
 
-        def add_residual_block(h, a):
+        def add_residual(h, a):
             result = kept["result", h]
-            nc.vector.tensor_add(out=result[:, a, :], in0=result[:, a, :], in1=x_tiles[h][:, a, :])
+            nc.vector.tensor_add(out=result[:, a, :], in0=result[:, a, :], in1=kept["x", h][:, a, :])
 
-        def store(h):
-            nc.sync.dma_start(out=out_rows[h // 2, :, out_slots(h), :], in_=kept["result", h][:])
+        def store(h, pair):
+            first = first_out_slot(h) + 2 * pair
+            nc.sync.dma_start(
+                out=out_rows[h // 2, :, first : first + 2, :],
+                in_=kept["result", h][:, 2 * pair : 2 * pair + 2, :],
+            )
 
-        def valid(h):
-            return 0 <= h < halves
+        def run(stage_of_half, h, *more):
+            if 0 <= h < halves:
+                stage_of_half(h, *more)
 
-        for i in range(FIRST_ROUND, halves + 2):
-            if valid(i + O_AHEAD):
-                load_o(i + O_AHEAD)
-            if valid(i + X_AHEAD):
-                load_x(i + X_AHEAD)
-            if valid(i + 3):
-                turn_half(i + 3)
-            if valid(i - 1):
-                squared_deviations(i - 1)
-            if valid(i + 2):
-                group_bank(i + 2, 0)
-            if valid(i - 1):
-                standard_deviation(i - 1)
-            if valid(i + 2):
-                group_bank(i + 2, 1)
-            if valid(i - 2):
-                normalise(i - 2)
-                finish_last_block(i - 2)
-            if valid(i):
-                new_projection(i)
-            for a in range(BLOCKS):
-                if valid(i):
-                    add_bias_block(i, a)
-                if valid(i + 1):
-                    project_block(i + 1, a)
-            for step in range(SLOPE_STEPS):
-                if valid(i - 1):
-                    slope_step(i - 1, step)
-                if step == 0 and valid(i + 2):
-                    quantise_half(i + 2)
-                if 1 <= step <= SHARED_BLOCKS and valid(i - 2):
-                    add_residual_block(i - 2, step - 1)
-            if valid(i - 2):
-                store(i - 2)
+        for i in range(FIRST_ROUND, halves + LAST_LAG):
+            run(load_o, i + O_AHEAD)
+            run(load_x, i + X_AHEAD)
+            run(turn_half, i + 2)
+            run(squared_deviations, i - 1)
+            run(group_bank, i + 1, 0)
+            run(standard_deviation, i - 1)
+            run(group_bank, i + 1, 1)
+            run(normalise, i - 2)
+            run(finish_last_block, i - 2)
+            run(add_bias, i)
+            run(slope_step, i - 1, 0)
+            run(quantise, i + 1, 0)
+            run(slope_step, i - 1, 1)
+            run(quantise, i + 1, 1)
+            run(project, i + 1)
+            run(slope_step, i - 1, 2)
+            run(add_residual, i - 2, 0)
+            run(slope_step, i - 1, 3)
+            run(add_residual, i - 2, 1)
+            run(store, i - 2, 0)
+            run(slope_step, i - 1, 4)
+            run(add_residual, i - 2, 2)
+            run(store, i - 2, 1)

@@ -22,6 +22,7 @@ BLOCKS = 4
 PAIRS = BLOCKS // 2
 EPS = 1e-5
 SHARED_BLOCKS = BLOCKS - 1
+SCALAR_BLOCKS = 2
 FIRST_ROUND = -2
 LAST_LAG = 2
 O_AHEAD = 5
@@ -257,7 +258,7 @@ def tile_swintransformerblock_pb_t_kernel(
 
         def normalise(h):
             result = work.tile([P, BLOCKS, C], F32)
-            for a in range(SHARED_BLOCKS):
+            for a in range(SCALAR_BLOCKS):
                 nc.scalar.activation(
                     out=result[:, a, :],
                     in_=kept["t", h][:, a, :],
@@ -266,6 +267,17 @@ def tile_swintransformerblock_pb_t_kernel(
                     scale=kept["slope", h][:, a : a + 1],
                 )
             kept["result", h] = result
+
+        def normalise_on_vector(h):
+            for a in range(SCALAR_BLOCKS, SHARED_BLOCKS):
+                nc.vector.tensor_scalar(
+                    out=kept["result", h][:, a, :],
+                    in0=kept["t", h][:, a, :],
+                    scalar1=kept["slope", h][:, a : a + 1],
+                    scalar2=kept["level", h][:, a : a + 1],
+                    op0=ALU.mult,
+                    op1=ALU.add,
+                )
 
         def finish_last_block(h):
             last = BLOCKS - 1
@@ -314,10 +326,11 @@ def tile_swintransformerblock_pb_t_kernel(
             run(quantise, i + 1, 1)
             run(project, i + 1)
             run(slope_step, i - 1, 2)
-            run(add_residual, i - 2, 0)
+            run(normalise_on_vector, i - 2)
             run(slope_step, i - 1, 3)
+            run(add_residual, i - 2, 0)
+            run(slope_step, i - 1, 4)
             run(add_residual, i - 2, 1)
             run(store, i - 2, 0)
-            run(slope_step, i - 1, 4)
             run(add_residual, i - 2, 2)
             run(store, i - 2, 1)

from contextlib import ExitStack

import concourse.mybir as mybir
from concourse.masks import make_identity

F32 = mybir.dt.float32
BF16 = mybir.dt.bfloat16
U32 = mybir.dt.uint32
U8 = mybir.dt.uint8
FP8X4 = mybir.dt.float8_e4m3fn_x4
ALU = mybir.AluOpType
ACT = mybir.ActivationFunctionType

P = 128
C = 512
IMAGES = 8
GRID = 32
WS = 8
NWIN = GRID // WS
SHIFT = 4
BLOCKS = 4
PAIRS = BLOCKS // 2
EPS = 1e-5
SHARED_BLOCKS = BLOCKS - 1
SCALAR_BLOCKS = 2
FIRST_ROUND = -2
LAST_LAG = 2
O_AHEAD = 5
X_AHEAD = 2
LOAD_BUFS = 6

FLOPS = 2 * IMAGES * GRID * GRID * C * C


def rolled(count, shift):
    pieces = [(0, shift, count - shift)]
    if shift:
        pieces.append((count - shift, 0, shift))
    return pieces


def make_window_permutation(nc, perm, ident, carry):
    dst = perm.rearrange("p (wi rh rl wj) -> p wi rh rl wj", wi=NWIN, rh=2, rl=SHIFT, wj=NWIN)
    src = ident.rearrange("p (wi wj rh rl) -> p wi rh rl wj", wi=NWIN, wj=NWIN, rh=2, rl=SHIFT)
    for rh in range(2):
        for wi_src, wi_dst, wi_len in rolled(NWIN, rh):
            for wj_src, wj_dst, wj_len in rolled(NWIN, carry):
                nc.vector.tensor_copy(
                    out=dst[:, wi_dst : wi_dst + wi_len, 1 - rh, :, wj_dst : wj_dst + wj_len],
                    in_=src[:, wi_src : wi_src + wi_len, rh, :, wj_src : wj_src + wj_len],
                )


def turn_rows(nc, turn, rows, perm):
    banks = []
    for pair in range(BLOCKS // 2):
        turned = turn.tile([P, 2, 2, P], F32)
        for a in range(2):
            words = rows[:, 2 * pair + a, :].bitcast(F32)
            for u in range(2):
                nc.tensor.transpose(turned[:, a, u, :], words[:, u * P : (u + 1) * P], perm)
        banks.append(turned)
    return banks


def group_words(copy_out, grouped, banks, pair):
    grouped_words = grouped[:].bitcast(F32).rearrange("p (a j u) -> p a j u", a=BLOCKS, u=2)
    copy_out(
        out=grouped_words[:, 2 * pair : 2 * pair + 2, :, :],
        in_=banks[pair][:].rearrange("p a u j -> p a j u"),
    )


def quantise_pair(nc, grouped, codes, scales, pair):
    cols = slice(2 * P * pair, 2 * P * (pair + 1))
    nc.vector.quantize_mx(
        out=codes[:, cols].bitcast(FP8X4),
        scales=scales[:, cols],
        in_=grouped[:, 2 * C * pair : 2 * C * (pair + 1)],
    )


def tile_swintransformerblock_pb_t_kernel(
    tc, o_attn, out_w, out_b, ada1_scale, ada1_shift, x, out
):
    nc = tc.nc
    halves = 2 * IMAGES

    o_rows = o_attn.flatten_outer_dims().rearrange("(b p c) k -> b p c k", p=P, c=WS)
    x_rows = x.rearrange("b (p s) n -> b p s n", s=WS)
    out_rows = out.rearrange("b (p s) n -> b p s n", s=WS)

    def first_out_slot(h):
        return BLOCKS * (1 - h % 2)

    def out_slots(h):
        return slice(first_out_slot(h), first_out_slot(h) + BLOCKS)

    with ExitStack() as stack:
        consts = stack.enter_context(tc.tile_pool(name="consts", bufs=1))
        loads = stack.enter_context(tc.tile_pool(name="loads", bufs=LOAD_BUFS))
        stage = stack.enter_context(tc.tile_pool(name="stage", bufs=2))
        work = stack.enter_context(tc.tile_pool(name="work", bufs=3))
        stats = stack.enter_context(tc.tile_pool(name="stats", bufs=4))
        turn = stack.enter_context(tc.psum_pool(name="turn", bufs=4))
        accs = stack.enter_context(tc.psum_pool(name="accs", bufs=4))
        stack.enter_context(tc.manual_schedule())

        kept = {}

        def load_o(h):
            o_tile = loads.tile([P, BLOCKS, C], BF16)
            first = BLOCKS * (h % 2)
            nc.sync.dma_start(out=o_tile[:], in_=o_rows[h // 2, :, first : first + BLOCKS, :])
            kept["o", h] = o_tile

        def load_x(h):
            x_tile = loads.tile([P, BLOCKS, C], BF16)
            nc.sync.dma_start(out=x_tile[:], in_=x_rows[h // 2, :, out_slots(h), :])
            kept["x", h] = x_tile

        w_rows = consts.tile([P, BLOCKS, C], BF16)
        nc.sync.dma_start(out=w_rows[:], in_=out_w.rearrange("(a p) k -> p a k", p=P))
        bias_row = consts.tile([P, C], BF16)
        nc.vector.memset(bias_row[:], 0.0)
        nc.sync.dma_start(out=bias_row[0:1, :], in_=out_b.rearrange("(o n) -> o n", o=1))
        for h in range(O_AHEAD + FIRST_ROUND):
            load_o(h)
        gain = consts.tile([P, WS], BF16)
        nc.sync.dma_start(
            out=gain[:], in_=ada1_scale.flatten_outer_dims().rearrange("(p s) q -> p (s q)", p=P)
        )
        offset = consts.tile([P, WS], BF16)
        nc.sync.dma_start(
            out=offset[:], in_=ada1_shift.flatten_outer_dims().rearrange("(p s) q -> p (s q)", p=P)
        )

        ones = consts.tile([P, P], BF16)
        nc.vector.memset(ones[:], 1.0)
        table_warmer = consts.tile([P, 1], F32)
        nc.scalar.activation(out=table_warmer[:], in_=ones[:, 0:1], func=ACT.Sqrt)

        ident = consts.tile([P, P], F32)
        make_identity(nc, ident[:])
        perms = []
        for carry in range(2):
            perm = consts.tile([P, P], F32, name="perm%d" % carry)
            make_window_permutation(nc, perm[:], ident[:], carry)
            perms.append(perm)

        w_codes = consts.tile([P, C], U32, align_bytes=64)
        w_scales = consts.tile([P, C], U8, align_bytes=64)
        w_banks = turn_rows(nc, turn, w_rows, ident[:])
        w_grouped = stage.tile([P, BLOCKS * C], BF16, align_bytes=64, tag="grouped")
        for pair in range(PAIRS):
            group_words(nc.vector.tensor_copy, w_grouped, w_banks, pair)
        for pair in range(PAIRS):
            quantise_pair(nc, w_grouped, w_codes, w_scales, pair)

        bias_bank = accs.tile([P, C], F32, tag="acc")
        nc.tensor.matmul(bias_bank[:], lhsT=ones[:], rhs=bias_row[:], start=True, stop=True)
        bias = consts.tile([P, C], F32)
        nc.vector.tensor_copy(out=bias[:], in_=bias_bank[:])

        def turn_half(h):
            kept["banks", h] = turn_rows(nc, turn, kept["o", h], perms[h % 2][:])

        def group_bank(h, pair):
            if pair == 0:
                grouped = stage.tile([P, BLOCKS * C], BF16, align_bytes=64, tag="grouped")
                kept["grouped", h] = grouped
            group_words(nc.scalar.copy, kept["grouped", h], kept["banks", h], pair)

        def quantise(h, pair):
            if pair == 0:
                o_codes = stage.tile([P, BLOCKS * P], U32, align_bytes=64)
                o_scales = stage.tile([P, BLOCKS * P], U8, align_bytes=64)
                kept["codes", h] = o_codes
                kept["scales", h] = o_scales
            quantise_pair(nc, kept["grouped", h], kept["codes", h], kept["scales", h], pair)

        def project(h):
            for a in range(BLOCKS):
                cols = slice(a * P, (a + 1) * P)
                acc = accs.tile([P, C], F32, tag="acc")
                nc.tensor.matmul_mx(
                    out=acc[:],
                    lhsT=kept["codes", h][:, cols].bitcast(FP8X4),
                    lhsT_scale=kept["scales", h][:, cols],
                    rhs=w_codes[:].bitcast(FP8X4),
                    rhs_scale=w_scales[:],
                    start=True,
                    stop=True,
                )
                kept["acc", h, a] = acc

        def add_bias(h):
            t_all = work.tile([P, BLOCKS, C], F32)
            t_sum = stats.tile([P, BLOCKS], F32)
            for a in range(BLOCKS):
                nc.vector.scalar_tensor_tensor(
                    out=t_all[:, a, :],
                    in0=kept["acc", h, a][:],
                    scalar=1.0,
                    in1=bias[:],
                    op0=ALU.mult,
                    op1=ALU.add,
                    accum_out=t_sum[:, a : a + 1],
                )
            kept["t", h] = t_all
            kept["t_sum", h] = t_sum

        def squared_deviations(h):
            squares = stage.tile([P, BLOCKS, C], BF16)
            dev_sq = stats.tile([P, BLOCKS], F32)
            for a in range(BLOCKS):
                nc.scalar.activation(
                    out=squares[:, a, :],
                    in_=kept["t", h][:, a, :],
                    func=ACT.Square,
                    bias=kept["t_sum", h][:, a : a + 1],
                    scale=-1.0 * C,
                    accum_out=dev_sq[:, a : a + 1],
                )
            kept["dev_sq", h] = dev_sq

        def standard_deviation(h):
            std = stats.tile([P, BLOCKS], F32)
            nc.scalar.activation(
                out=std[:], in_=kept["dev_sq", h][:], func=ACT.Sqrt, scale=1.0 / ((C - 1) * C * C)
            )
            kept["std", h] = std

        def slope_step(h, step):
            if step == 0:
                slope = stats.tile([P, BLOCKS], F32)
                level = stats.tile([P, BLOCKS], F32)
                kept["slope", h] = slope
                kept["level", h] = level
                nc.vector.tensor_scalar_add(out=slope[:], in0=kept["std", h][:], scalar1=EPS)
            slope = kept["slope", h]
            level = kept["level", h]
            if step == 1:
                nc.vector.reciprocal(out=slope[:], in_=slope[:])
            if step == 2:
                nc.vector.tensor_mul(out=slope[:], in0=slope[:], in1=gain[:, out_slots(h)])
            if step == 3:
                nc.vector.tensor_mul(out=level[:], in0=kept["t_sum", h][:], in1=slope[:])
            if step == 4:
                nc.vector.scalar_tensor_tensor(
                    out=level[:],
                    in0=level[:],
                    scalar=-1.0 / C,
                    in1=offset[:, out_slots(h)],
                    op0=ALU.mult,
                    op1=ALU.add,
                )

        def normalise(h):
            result = work.tile([P, BLOCKS, C], F32)
            for a in range(SCALAR_BLOCKS):
                nc.scalar.activation(
                    out=result[:, a, :],
                    in_=kept["t", h][:, a, :],
                    func=ACT.Identity,
                    bias=kept["level", h][:, a : a + 1],
                    scale=kept["slope", h][:, a : a + 1],
                )
            kept["result", h] = result

        def normalise_on_vector(h):
            for a in range(SCALAR_BLOCKS, SHARED_BLOCKS):
                nc.vector.tensor_scalar(
                    out=kept["result", h][:, a, :],
                    in0=kept["t", h][:, a, :],
                    scalar1=kept["slope", h][:, a : a + 1],
                    scalar2=kept["level", h][:, a : a + 1],
                    op0=ALU.mult,
                    op1=ALU.add,
                )

        def finish_last_block(h):
            last = BLOCKS - 1
            result = kept["result", h]
            nc.gpsimd.tensor_scalar(
                out=result[:, last, :],
                in0=kept["t", h][:, last, :],
                scalar1=kept["slope", h][:, last : last + 1],
                scalar2=kept["level", h][:, last : last + 1],
                op0=ALU.mult,
                op1=ALU.add,
            )
            nc.gpsimd.tensor_add(
                out=result[:, last, :], in0=result[:, last, :], in1=kept["x", h][:, last, :]
            )

        def add_residual(h, a):
            result = kept["result", h]
            nc.vector.tensor_add(out=result[:, a, :], in0=result[:, a, :], in1=kept["x", h][:, a, :])

        def store(h, pair):
            first = first_out_slot(h) + 2 * pair
            nc.sync.dma_start(
                out=out_rows[h // 2, :, first : first + 2, :],
                in_=kept["result", h][:, 2 * pair : 2 * pair + 2, :],
            )

        def run(stage_of_half, h, *more):
            if 0 <= h < halves:
                stage_of_half(h, *more)

        for i in range(FIRST_ROUND, halves + LAST_LAG):
            run(load_o, i + O_AHEAD)
            run(load_x, i + X_AHEAD)
            run(turn_half, i + 2)
            run(squared_deviations, i - 1)
            run(group_bank, i + 1, 0)
            run(standard_deviation, i - 1)
            run(group_bank, i + 1, 1)
            run(normalise, i - 2)
            run(finish_last_block, i - 2)
            run(add_bias, i)
            run(slope_step, i - 1, 0)
            run(quantise, i + 1, 0)
            run(slope_step, i - 1, 1)
            run(quantise, i + 1, 1)
            run(project, i + 1)
            run(slope_step, i - 1, 2)
            run(normalise_on_vector, i - 2)
            run(slope_step, i - 1, 3)
            run(add_residual, i - 2, 0)
            run(slope_step, i - 1, 4)
            run(add_residual, i - 2, 1)
            run(store, i - 2, 0)
            run(add_residual, i - 2, 2)
            run(store, i - 2, 1)
